import numpy as np
import ml_dtypes


def mxq(x, axis, fmt="e4m3"):
    dtype, down = {"e4m3": (ml_dtypes.float8_e4m3fn, 7), "e5m2": (ml_dtypes.float8_e5m2, 14)}[fmt]
    v = np.moveaxis(np.asarray(x, np.float32).astype(ml_dtypes.bfloat16).astype(np.float64), axis, -1)
    blocks = v.reshape(v.shape[:-1] + (-1, 32))
    amax = np.abs(blocks).max(-1, keepdims=True)
    byte = np.maximum(np.where(amax > 0, np.frexp(amax)[1] - 1 + 127, 0) - down, 1)
    scale = np.exp2(byte - 127.0)
    codes = (blocks / scale).astype(np.float32).astype(dtype).astype(np.float64)
    return np.moveaxis((codes * scale).reshape(v.shape), -1, axis)


WIDE = False


def mx_kscale(k):
    if not WIDE:
        return np.ones(k)
    levels = np.array([30, -30])
    if k % 512:
        return np.exp2(np.random.permutation(np.resize(levels, k // 32))).repeat(32)
    a = np.empty((k // 512, 16))
    for p in range(k // 512):
        a[p, :8] = np.random.permutation(np.resize(levels, 8))
        for g in range(8):
            far = levels[np.abs(levels - a[p, g]) >= 10]
            a[p, g + 8] = far[np.random.randint(len(far))]
    return np.exp2(a.ravel()).repeat(32)


BF16 = ml_dtypes.bfloat16


def bf(x):
    return np.asarray(x, np.float32).astype(BF16)


def f64(x):
    return np.asarray(x).astype(np.float64)


E2M1 = np.array([0.0, 0.5, 1.0, 1.5, 2.0, 3.0, 4.0, 6.0, -0.0, -0.5, -1.0, -1.5, -2.0, -3.0, -4.0, -6.0])


def pack_weight(w, fmt):
    k, n = w.shape
    w = f64(bf(w)).reshape(k // 32, 32, n)
    amax = np.abs(w).max(1)
    if fmt == "e4m3":
        byte = np.frexp(amax)[1] - 1 + 127 - 7
    else:
        mant, ex = np.frexp(amax / 6.0)
        byte = np.where(mant > 0.5, ex, ex - 1) + 127
    byte = np.clip(np.where(amax > 0, byte, 1), 1, 254)
    scaled = (w * np.exp2(127.0 - byte)[:, None, :]).reshape(k, n).astype(np.float32)
    by_word = np.ascontiguousarray(scaled.reshape(k // 512, 128, 4, n).transpose(0, 1, 3, 2))
    if fmt == "e4m3":
        words = by_word.astype(ml_dtypes.float8_e4m3fn).view(np.uint8)
    else:
        c = by_word.astype(ml_dtypes.float4_e2m1fn).view(np.uint8) & 0xF
        words = c[..., 0::2] | (c[..., 1::2] << 4)
    return np.ascontiguousarray(words), np.ascontiguousarray(byte.astype(np.uint8).reshape(k // 512, 16, n))


def unpack_weight(words, scales, fmt):
    g, p, n, _ = words.shape
    if fmt == "e4m3":
        vals = np.ascontiguousarray(words).view(ml_dtypes.float8_e4m3fn).astype(np.float64)
    else:
        nib = np.empty((g, p, n, 4), np.uint8)
        nib[..., 0::2] = words & 0xF
        nib[..., 1::2] = words >> 4
        vals = E2M1[nib]
    vals = vals * np.repeat(np.exp2(scales.astype(np.float64) - 127.0), 8, axis=1)[..., None]
    return vals.transpose(0, 1, 3, 2).reshape(g * 512, n)

def pack4(w):
    words, scales = pack_weight(w, "e2m1")
    return words.reshape(words.shape[0], 128, -1), scales


def unpack4(words, scales):
    return unpack_weight(words.reshape(words.shape[0], 128, -1, 2), scales, "e2m1")


B, N, D, H, DH = 2, 512, 1024, 16, 64
INNER = H * DH


def dpfp(u):
    u2 = np.concatenate([np.maximum(u, 0.0), np.maximum(-u, 0.0)], axis=-1)
    return u2 * np.roll(u2, 1, axis=-1)


def heads(t):
    return t.reshape(B, N, H, DH).transpose(0, 2, 1, 3)


def setup_inputs():
    s = mx_kscale(D)
    x = bf(np.random.standard_normal((B, N, D)) * s)
    words, scales = pack4(np.random.standard_normal((D, 2 * INNER)) / np.sqrt(D) / s[:, None])
    return {"x": x, "w_qk_words": words, "w_qk_scales": scales}


def reference(x, w_qk_words, w_qk_scales):
    qk = mxq(f64(x), 2, "e5m2") @ unpack4(w_qk_words, w_qk_scales)
    q, k = np.split(qk, 2, axis=-1)
    q, k = dpfp(heads(q)), dpfp(heads(k))
    return q / q.sum(-1, keepdims=True), k / k.sum(-1, keepdims=True)

@@ -1,0 +1,300 @@
+from contextlib import ExitStack
+
+import concourse.mybir as mybir
+from concourse.masks import make_identity
+
+B, N, D, H, DH = 2, 512, 1024, 16, 64
+FLOPS = 2 * B * N * D * 2 * H * DH
+
+F32 = mybir.dt.float32
+BF16 = mybir.dt.bfloat16
+U32 = mybir.dt.uint32
+U8 = mybir.dt.uint8
+I32 = mybir.dt.int32
+E5M2X4 = mybir.dt.float8_e5m2_x4
+E2M1X4 = mybir.dt.float4_e2m1fn_x4
+ACT = mybir.ActivationFunctionType
+ALU = mybir.AluOpType
+AX = mybir.AxisListType
+
+P = 128
+J = 4
+NG = D // 512
+HB = 8
+NCG = 2 * H // HB
+NU = B * NCG * J
+CHUNKS = (2, 4, 4, 4, 4, 4, 2, 1)
+V_FINAL = 1
+LEAD_MM = 3
+LEAD_SG = 2
+
+
+def tile_dpfpattention_pa_kernel(tc, x, w_qk_words, w_qk_scales, out_0, out_1):
+    nc = tc.nc
+    with ExitStack() as ctx:
+        const = ctx.enter_context(tc.tile_pool(name="const", bufs=1))
+        stage = ctx.enter_context(tc.tile_pool(name="stage", bufs=2))
+        work = ctx.enter_context(tc.tile_pool(name="work", bufs=3))
+        outp = ctx.enter_context(tc.tile_pool(name="outp", bufs=3))
+        psum_t = ctx.enter_context(tc.psum_pool(name="psum_t", bufs=2))
+        psum_u = ctx.enter_context(tc.psum_pool(name="psum_u", bufs=6))
+
+        x_sb, xq, xs, grouped = {}, {}, {}, {}
+        ww, ws = {}, {}
+        u_ps, sg, cp, tp, tn, rc, sm, o_sb = {}, {}, {}, {}, {}, {}, {}, {}
+
+        zero = const.tile([P, 1], F32, name="zero")
+        nc.vector.memset(zero[:], 0.0)
+        warm = const.tile([P, 1], F32, name="warm")
+        nc.scalar.activation(out=warm[:], in_=zero[:], func=ACT.Sign)
+
+        for cg in range(NCG):
+            plane = const.tile([P, NG, 512], U8, name="ws%d" % cg, align_bytes=64)
+            nc.vector.memset(plane[:].bitcast(I32), 0)
+            ws[cg] = plane
+
+        ident = const.tile([P, P], F32, name="ident")
+        make_identity(nc, ident[:])
+
+        def load_x(t):
+            b, j = divmod(t, J)
+            xt = const.tile([P, D], BF16, name="x%d" % t)
+            nc.sync.dma_start(out=xt[:], in_=x[b].rearrange("(p j) k -> p j k", j=J)[:, j, :])
+            x_sb[t] = xt
+
+        def load_w(cg):
+            for q in range(4):
+                nc.sync.dma_start(
+                    out=ws[cg][32 * q : 32 * q + 4, :, :].bitcast(I32),
+                    in_=w_qk_scales[:, 4 * q : 4 * q + 4, 512 * cg : 512 * (cg + 1)]
+                    .rearrange("g r n -> r g n")
+                    .bitcast(I32),
+                )
+            words = const.tile([P, NG, 1024], U8, name="ww%d" % cg, align_bytes=64)
+            nc.sync.dma_start(
+                out=words[:].bitcast(I32),
+                in_=w_qk_words[:, :, 1024 * cg : 1024 * (cg + 1)].rearrange("g p n -> p g n").bitcast(I32),
+            )
+            ww[cg] = words
+
+        load_x(0)
+        load_w(0)
+        for t in range(1, B * J):
+            load_x(t)
+        load_w(1)
+        load_w(2)
+        load_w(3)
+
+        def prep(t):
+            words = x_sb[t][:].bitcast(F32)
+            xT = psum_t.tile([P, 2 * NG, P], F32, name="xT")
+            for g in range(NG):
+                for u in range(2):
+                    nc.tensor.transpose(xT[:, 2 * g + u, :], words[:, 256 * g + u : 256 * (g + 1) : 2], ident[:])
+            gr = stage.tile([P, NG * 512], BF16, name="gr", align_bytes=64)
+            nc.scalar.copy(
+                out=gr[:].bitcast(F32).rearrange("p (g r u) -> p g r u", g=NG, u=2),
+                in_=xT[:].rearrange("p (g u) r -> p g r u", u=2),
+            )
+            grouped[t] = gr
+
+        def quant(t):
+            codes = const.tile([P, NG * P], U32, name="xq%d" % t, align_bytes=64)
+            scales = const.tile([P, NG * P], U8, name="xs%d" % t, align_bytes=64)
+            nc.vector.quantize_mx(out=codes[:].bitcast(E5M2X4), scales=scales[:], in_=grouped[t][:])
+            xq[t] = codes
+            xs[t] = scales
+
+        def where(n):
+            b, rest = divmod(n, NCG * J)
+            cg, j = divmod(rest, J)
+            return b, cg, j
+
+        def mm(n):
+            b, cg, j = where(n)
+            t = J * b + j
+            acc = psum_u.tile([P, 512], F32, name="acc")
+            for g in range(NG):
+                nc.tensor.matmul_mx(
+                    out=acc[:],
+                    lhsT=xq[t][:, P * g : P * (g + 1)].bitcast(E5M2X4),
+                    lhsT_scale=xs[t][:, P * g : P * (g + 1)],
+                    rhs=ww[cg][:, g, :].bitcast(E2M1X4),
+                    rhs_scale=ws[cg][:, g, :],
+                    start=(g == 0),
+                    stop=(g == NG - 1),
+                )
+            u_ps[n] = acc
+
+        def sign(n):
+            s = work.tile([P, 512], F32, name="sg", bufs=5)
+            nc.scalar.activation(out=s[:], in_=u_ps[n][:], func=ACT.Sign)
+            sg[n] = s
+
+        def heads(ap):
+            return ap.rearrange("p (h i) -> p h i", i=DH)
+
+        def c_main(n):
+            c = work.tile([P, 512], F32, name="cp")
+            cp[n] = c
+            nc.vector.tensor_tensor(
+                out=heads(c[:])[:, :, 1:DH],
+                in0=heads(u_ps[n][:])[:, :, 0 : DH - 1],
+                in1=heads(sg[n][:])[:, :, 1:DH],
+                op=ALU.mult,
+            )
+
+        def c_wrap(n):
+            nc.vector.scalar_tensor_tensor(
+                out=heads(cp[n][:])[:, :, 0:1],
+                in0=heads(u_ps[n][:])[:, :, DH - 1 : DH],
+                scalar=-1.0,
+                in1=heads(sg[n][:])[:, :, 0:1],
+                op0=ALU.mult,
+                op1=ALU.mult,
+            )
+
+        chunk_of = {}
+        last_of = {}
+        for grp in range(NU // J):
+            size = CHUNKS[grp]
+            for first in range(J * grp, J * (grp + 1), size):
+                last_of[first + size - 1] = (first, size)
+                for n in range(first, first + size):
+                    chunk_of[n] = (first, size)
+
+        def t_prime(n):
+            first, size = chunk_of[n]
+            if n == first:
+                tpt = work.tile([P, size, 512], F32, name="tp")
+                tp[first] = tpt
+            nc.vector.scalar_tensor_tensor(
+                out=tp[first][:, n - first, :],
+                in0=cp[n][:],
+                scalar=0.0,
+                in1=u_ps[n][:],
+                op0=ALU.max,
+                op1=ALU.mult,
+            )
+
+        def reduce(first, size):
+            s = work.tile([P, size * HB], F32, name="sm")
+            nc.vector.tensor_reduce(
+                out=s[:],
+                in_=tp[first][:].rearrange("p j (h i) -> p (j h) i", i=DH),
+                axis=AX.X,
+                op=ALU.add,
+                apply_absolute_value=True,
+            )
+            sm[first] = s
+
+        def recip(first, size):
+            r = work.tile([P, size * HB], F32, name="rc")
+            nc.vector.reciprocal(out=r[:], in_=sm[first][:])
+            rc[first] = r
+
+        def spread(r_ap):
+            return r_ap.unsqueeze(2).to_broadcast([P, HB, DH])
+
+        def scale(first, size):
+            t = work.tile([P, size, 512], F32, name="tn")
+            tn[first] = t
+            for k in range(size):
+                nc.gpsimd.tensor_tensor(
+                    out=heads(t[:, k, :]),
+                    in0=heads(tp[first][:, k, :]),
+                    in1=spread(rc[first][:, HB * k : HB * (k + 1)]),
+                    op=ALU.mult,
+                )
+
+        def out_tile(n):
+            grp, j = divmod(n, J)
+            if j == 0:
+                o = outp.tile([P, HB, J, 2 * DH], F32, name="o")
+                o_sb[grp] = o
+            return o_sb[grp], j
+
+        def relus(n):
+            o, j = out_tile(n)
+            first, size = chunk_of[n]
+            src = heads(tn[first][:, n - first, :])
+            nc.scalar.activation(out=o[:, :, j, 0:DH], in_=src, func=ACT.Relu)
+            nc.scalar.activation(out=o[:, :, j, DH : 2 * DH], in_=src, func=ACT.Relu, scale=-1.0)
+
+        def v_final(n):
+            o, j = out_tile(n)
+            first, size = chunk_of[n]
+            src = heads(tp[first][:, n - first, :])
+            r = rc[first][:, HB * (n - first) : HB * (n - first + 1)]
+            rneg = work.tile([P, HB], F32, name="rneg")
+            nc.vector.tensor_scalar(out=rneg[:], in0=r, scalar1=-1.0, scalar2=None, op0=ALU.mult)
+            nc.vector.scalar_tensor_tensor(
+                out=o[:, :, j, 0:DH], in0=src, scalar=0.0, in1=spread(r), op0=ALU.max, op1=ALU.mult
+            )
+            nc.vector.scalar_tensor_tensor(
+                out=o[:, :, j, DH : 2 * DH], in0=src, scalar=0.0, in1=spread(rneg[:]), op0=ALU.min, op1=ALU.mult
+            )
+
+        def dest(grp):
+            b, cg = divmod(grp, NCG)
+            dst = out_0 if cg < NCG // 2 else out_1
+            h0 = HB * (cg % (NCG // 2))
+            return dst, b, h0
+
+        def store(first, size, h_lo, h_n):
+            grp, j = divmod(first, J)
+            dst, b, h0 = dest(grp)
+            nc.sync.dma_start(
+                out=dst[b, h0 + h_lo : h0 + h_lo + h_n]
+                .rearrange("h (p j) f -> p h j f", j=J)[:, :, j : j + size, :]
+                .rearrange("p h j f -> p h (j f)"),
+                in_=o_sb[grp][:, h_lo : h_lo + h_n, j : j + size, :].rearrange("p h j f -> p h (j f)"),
+            )
+
+        def finish(n):
+            if n >= NU - V_FINAL:
+                v_final(n)
+            else:
+                relus(n)
+            if n in last_of:
+                first, size = last_of[n]
+                store(first, size, 0, HB // 2)
+                store(first, size, HB // 2, HB // 2)
+
+        for t in range(LEAD_MM):
+            prep(t)
+            quant(t)
+        for n in range(LEAD_MM):
+            mm(n)
+        for n in range(LEAD_SG):
+            sign(n)
+        pending = []
+        served = 0
+        for n in range(NU + 2):
+            if n + LEAD_MM < B * J:
+                prep(n + LEAD_MM)
+                quant(n + LEAD_MM)
+            if n + LEAD_MM < NU:
+                mm(n + LEAD_MM)
+            if n + LEAD_SG < NU:
+                sign(n + LEAD_SG)
+            if n < NU:
+                c_main(n)
+            ready = last_of.get(n - 2)
+            if ready:
+                reduce(ready[0], ready[1])
+            if 1 <= n <= NU:
+                t_prime(n - 1)
+            if n < NU:
+                c_wrap(n)
+            for k in range(2 if len(pending) - served > J else 1):
+                if served < len(pending):
+                    finish(pending[served])
+                    served += 1
+            if ready:
+                recip(ready[0], ready[1])
+                if ready[0] < NU - V_FINAL:
+                    scale(ready[0], ready[1])
+                pending.extend(range(ready[0], ready[0] + ready[1]))
+        for n in pending[served:]:
+            finish(n)

@@ -41,7 +41,7 @@ def tile_dpfpattention_pa_kernel(tc, x, w_qk_words, w_qk_scales, out_0, out_1):
 
         x_sb, xq, xs, grouped = {}, {}, {}, {}
         ww, ws = {}, {}
-        u_ps, sg, cp, tp, tn, rc, sm, o_sb = {}, {}, {}, {}, {}, {}, {}, {}
+        u_ps, sg, cp, tp, tn, rc, rn, sm, o_sb = {}, {}, {}, {}, {}, {}, {}, {}, {}
 
         zero = const.tile([P, 1], F32, name="zero")
         nc.vector.memset(zero[:], 0.0)
@@ -192,6 +192,9 @@ def tile_dpfpattention_pa_kernel(tc, x, w_qk_words, w_qk_scales, out_0, out_1):
             r = work.tile([P, size * HB], F32, name="rc")
             nc.vector.reciprocal(out=r[:], in_=sm[first][:])
             rc[first] = r
+            rm = work.tile([P, size * HB], F32, name="rn")
+            nc.vector.tensor_scalar(out=rm[:], in0=r[:], scalar1=-1.0, scalar2=None, op0=ALU.mult)
+            rn[first] = rm
 
         def spread(r_ap):
             return r_ap.unsqueeze(2).to_broadcast([P, HB, DH])
@@ -217,22 +220,26 @@ def tile_dpfpattention_pa_kernel(tc, x, w_qk_words, w_qk_scales, out_0, out_1):
         def relus(n):
             o, j = out_tile(n)
             first, size = chunk_of[n]
-            src = heads(tn[first][:, n - first, :])
-            nc.scalar.activation(out=o[:, :, j, 0:DH], in_=src, func=ACT.Relu)
-            nc.scalar.activation(out=o[:, :, j, DH : 2 * DH], in_=src, func=ACT.Relu, scale=-1.0)
+            k = n - first
+            for h in range(HB):
+                src = tp[first][:, k, DH * h : DH * (h + 1)]
+                c = HB * k + h
+                nc.scalar.activation(out=o[:, h, j, 0:DH], in_=src, func=ACT.Relu, scale=rc[first][:, c : c + 1])
+                nc.scalar.activation(
+                    out=o[:, h, j, DH : 2 * DH], in_=src, func=ACT.Relu, scale=rn[first][:, c : c + 1]
+                )
 
         def v_final(n):
             o, j = out_tile(n)
             first, size = chunk_of[n]
             src = heads(tp[first][:, n - first, :])
             r = rc[first][:, HB * (n - first) : HB * (n - first + 1)]
-            rneg = work.tile([P, HB], F32, name="rneg")
-            nc.vector.tensor_scalar(out=rneg[:], in0=r, scalar1=-1.0, scalar2=None, op0=ALU.mult)
+            rneg = rn[first][:, HB * (n - first) : HB * (n - first + 1)]
             nc.vector.scalar_tensor_tensor(
                 out=o[:, :, j, 0:DH], in0=src, scalar=0.0, in1=spread(r), op0=ALU.max, op1=ALU.mult
             )
             nc.vector.scalar_tensor_tensor(
-                out=o[:, :, j, DH : 2 * DH], in0=src, scalar=0.0, in1=spread(rneg[:]), op0=ALU.min, op1=ALU.mult
+                out=o[:, :, j, DH : 2 * DH], in0=src, scalar=0.0, in1=spread(rneg), op0=ALU.min, op1=ALU.mult
             )
 
         def dest(grp):
@@ -293,8 +300,6 @@ def tile_dpfpattention_pa_kernel(tc, x, w_qk_words, w_qk_scales, out_0, out_1):
                     served += 1
             if ready:
                 recip(ready[0], ready[1])
-                if ready[0] < NU - V_FINAL:
-                    scale(ready[0], ready[1])
                 pending.extend(range(ready[0], ready[0] + ready[1]))
         for n in pending[served:]:
             finish(n)

@@ -22,34 +22,47 @@ J = 4
 NG = D // 512
 HB = 8
 NCG = 2 * H // HB
-NU = B * NCG * J
-CHUNKS = (2, 4, 4, 4, 4, 4, 2, 1)
+BANK = HB * DH
+CHUNK = 2
 V_FINAL = 1
-LEAD_MM = 3
-LEAD_SG = 2
+LEAD_MM = 4
+LEAD_SG = 3
+N_WARM = 4
+STORE_SPLIT = 4
+
+
+def unit_order():
+    units = [(0, cg, j) for j in range(J) for cg in (0, 1)]
+    units += [(0, cg, j) for cg in (2, 3) for j in range(J)]
+    units += [(1, cg, j) for cg in range(NCG) for j in range(J)]
+    return units
 
 
 def tile_dpfpattention_pa_kernel(tc, x, w_qk_words, w_qk_scales, out_0, out_1):
     nc = tc.nc
+    units = unit_order()
+    nu = len(units)
+    rows = {(b, cg): J for b in range(B) for cg in range(NCG)}
+    rows[(1, 2)] = 2
+    rows[(1, 3)] = 2
     with ExitStack() as ctx:
         const = ctx.enter_context(tc.tile_pool(name="const", bufs=1))
-        stage = ctx.enter_context(tc.tile_pool(name="stage", bufs=2))
-        work = ctx.enter_context(tc.tile_pool(name="work", bufs=3))
-        outp = ctx.enter_context(tc.tile_pool(name="outp", bufs=3))
-        psum_t = ctx.enter_context(tc.psum_pool(name="psum_t", bufs=2))
-        psum_u = ctx.enter_context(tc.psum_pool(name="psum_u", bufs=6))
+        stage = ctx.enter_context(tc.tile_pool(name="stage", bufs=3))
+        work = ctx.enter_context(tc.tile_pool(name="work", bufs=4))
+        outp = ctx.enter_context(tc.tile_pool(name="outp", bufs=4))
+        psum = ctx.enter_context(tc.psum_pool(name="psum", bufs=8))
 
         x_sb, xq, xs, grouped = {}, {}, {}, {}
         ww, ws = {}, {}
-        u_ps, sg, cp, tp, tn, rc, rn, sm, o_sb = {}, {}, {}, {}, {}, {}, {}, {}, {}
+        u_ps, sg, cp, tp, tn, rc, sm, o_sb = {}, {}, {}, {}, {}, {}, {}, {}
 
-        zero = const.tile([P, 1], F32, name="zero")
+        zero = const.tile([P, BANK], BF16, name="zero")
         nc.vector.memset(zero[:], 0.0)
         warm = const.tile([P, 1], F32, name="warm")
-        nc.scalar.activation(out=warm[:], in_=zero[:], func=ACT.Sign)
+        nc.scalar.activation(out=warm[:], in_=zero[:, 0:1], func=ACT.Sign)
 
         for cg in range(NCG):
-            plane = const.tile([P, NG, 512], U8, name="ws%d" % cg, align_bytes=64)
+            plane = const.tile([P, NG, BANK], U8, name="ws%d" % cg, align_bytes=64)
             nc.vector.memset(plane[:].bitcast(I32), 0)
             ws[cg] = plane
 
@@ -66,28 +79,33 @@ def tile_dpfpattention_pa_kernel(tc, x, w_qk_words, w_qk_scales, out_0, out_1):
             for q in range(4):
                 nc.sync.dma_start(
                     out=ws[cg][32 * q : 32 * q + 4, :, :].bitcast(I32),
-                    in_=w_qk_scales[:, 4 * q : 4 * q + 4, 512 * cg : 512 * (cg + 1)]
+                    in_=w_qk_scales[:, 4 * q : 4 * q + 4, BANK * cg : BANK * (cg + 1)]
                     .rearrange("g r n -> r g n")
                     .bitcast(I32),
                 )
-            words = const.tile([P, NG, 1024], U8, name="ww%d" % cg, align_bytes=64)
+            words = const.tile([P, NG, 2 * BANK], U8, name="ww%d" % cg, align_bytes=64)
             nc.sync.dma_start(
                 out=words[:].bitcast(I32),
-                in_=w_qk_words[:, :, 1024 * cg : 1024 * (cg + 1)].rearrange("g p n -> p g n").bitcast(I32),
+                in_=w_qk_words[:, :, 2 * BANK * cg : 2 * BANK * (cg + 1)].rearrange("g p n -> p g n").bitcast(I32),
             )
             ww[cg] = words
 
         load_x(0)
         load_w(0)
-        for t in range(1, B * J):
-            load_x(t)
+        load_x(1)
         load_w(1)
+        for t in range(2, B * J):
+            load_x(t)
         load_w(2)
         load_w(3)
 
+        dummy = psum.tile([P, BANK], F32, name="bank")
+        for i in range(N_WARM):
+            nc.tensor.matmul(out=dummy[:], lhsT=zero[:, 0:P], rhs=zero[:], start=True, stop=True)
+
         def prep(t):
             words = x_sb[t][:].bitcast(F32)
-            xT = psum_t.tile([P, 2 * NG, P], F32, name="xT")
+            xT = psum.tile([P, 2 * NG, P], F32, name="bank")
             for g in range(NG):
                 for u in range(2):
                     nc.tensor.transpose(xT[:, 2 * g + u, :], words[:, 256 * g + u : 256 * (g + 1) : 2], ident[:])
@@ -105,15 +123,10 @@ def tile_dpfpattention_pa_kernel(tc, x, w_qk_words, w_qk_scales, out_0, out_1):
             xq[t] = codes
             xs[t] = scales
 
-        def where(n):
-            b, rest = divmod(n, NCG * J)
-            cg, j = divmod(rest, J)
-            return b, cg, j
-
         def mm(n):
-            b, cg, j = where(n)
+            b, cg, j = units[n]
             t = J * b + j
-            acc = psum_u.tile([P, 512], F32, name="acc")
+            acc = psum.tile([P, BANK], F32, name="bank")
             for g in range(NG):
                 nc.tensor.matmul_mx(
                     out=acc[:],
@@ -127,7 +140,7 @@ def tile_dpfpattention_pa_kernel(tc, x, w_qk_words, w_qk_scales, out_0, out_1):
             u_ps[n] = acc
 
         def sign(n):
-            s = work.tile([P, 512], F32, name="sg", bufs=5)
+            s = work.tile([P, BANK], F32, name="sg", bufs=LEAD_SG + 3)
             nc.scalar.activation(out=s[:], in_=u_ps[n][:], func=ACT.Sign)
             sg[n] = s
 
@@ -135,13 +148,10 @@ def tile_dpfpattention_pa_kernel(tc, x, w_qk_words, w_qk_scales, out_0, out_1):
             return ap.rearrange("p (h i) -> p h i", i=DH)
 
         def c_main(n):
-            c = work.tile([P, 512], F32, name="cp")
+            c = work.tile([P, BANK], F32, name="cp")
             cp[n] = c
             nc.vector.tensor_tensor(
-                out=heads(c[:])[:, :, 1:DH],
-                in0=heads(u_ps[n][:])[:, :, 0 : DH - 1],
-                in1=heads(sg[n][:])[:, :, 1:DH],
-                op=ALU.mult,
+                out=c[:, 1:BANK], in0=u_ps[n][:, 0 : BANK - 1], in1=sg[n][:, 1:BANK], op=ALU.mult
             )
 
         def c_wrap(n):
@@ -154,19 +164,10 @@ def tile_dpfpattention_pa_kernel(tc, x, w_qk_words, w_qk_scales, out_0, out_1):
                 op1=ALU.mult,
             )
 
-        chunk_of = {}
-        last_of = {}
-        for grp in range(NU // J):
-            size = CHUNKS[grp]
-            for first in range(J * grp, J * (grp + 1), size):
-                last_of[first + size - 1] = (first, size)
-                for n in range(first, first + size):
-                    chunk_of[n] = (first, size)
-
         def t_prime(n):
-            first, size = chunk_of[n]
+            first = n - n % CHUNK
             if n == first:
-                tpt = work.tile([P, size, 512], F32, name="tp")
+                tpt = work.tile([P, CHUNK, BANK], F32, name="tp")
                 tp[first] = tpt
             nc.vector.scalar_tensor_tensor(
                 out=tp[first][:, n - first, :],
@@ -177,129 +178,139 @@ def tile_dpfpattention_pa_kernel(tc, x, w_qk_words, w_qk_scales, out_0, out_1):
                 op1=ALU.mult,
             )
 
-        def reduce(first, size):
-            s = work.tile([P, size * HB], F32, name="sm")
+        def reduce(first):
+            s = work.tile([P, CHUNK * HB], F32, name="sm")
             nc.vector.tensor_reduce(
                 out=s[:],
-                in_=tp[first][:].rearrange("p j (h i) -> p (j h) i", i=DH),
+                in_=tp[first][:].rearrange("p k (h i) -> p (k h) i", i=DH),
                 axis=AX.X,
                 op=ALU.add,
                 apply_absolute_value=True,
             )
             sm[first] = s
 
-        def recip(first, size):
-            r = work.tile([P, size * HB], F32, name="rc")
+        def recip(first):
+            r = work.tile([P, CHUNK * HB], F32, name="rc")
             nc.vector.reciprocal(out=r[:], in_=sm[first][:])
             rc[first] = r
-            rm = work.tile([P, size * HB], F32, name="rn")
-            nc.vector.tensor_scalar(out=rm[:], in0=r[:], scalar1=-1.0, scalar2=None, op0=ALU.mult)
-            rn[first] = rm
 
-        def spread(r_ap):
-            return r_ap.unsqueeze(2).to_broadcast([P, HB, DH])
+        def spread(r_ap, nh):
+            return r_ap.unsqueeze(2).to_broadcast([P, nh, DH])
 
-        def scale(first, size):
-            t = work.tile([P, size, 512], F32, name="tn")
-            tn[first] = t
-            for k in range(size):
-                nc.gpsimd.tensor_tensor(
-                    out=heads(t[:, k, :]),
-                    in0=heads(tp[first][:, k, :]),
-                    in1=spread(rc[first][:, HB * k : HB * (k + 1)]),
-                    op=ALU.mult,
-                )
+        def scale(n):
+            first = n - n % CHUNK
+            k = n - first
+            if first not in tn:
+                t = work.tile([P, CHUNK, BANK], F32, name="tn")
+                tn[first] = t
+            nc.gpsimd.tensor_tensor(
+                out=heads(tn[first][:, k, :]),
+                in0=heads(tp[first][:, k, :]),
+                in1=spread(rc[first][:, HB * k : HB * (k + 1)], HB),
+                op=ALU.mult,
+            )
 
         def out_tile(n):
-            grp, j = divmod(n, J)
+            b, cg, j = units[n]
             if j == 0:
                 o = outp.tile([P, HB, J, 2 * DH], F32, name="o")
-                o_sb[grp] = o
-            return o_sb[grp], j
+                o_sb[(b, cg)] = o
+            return o_sb[(b, cg)], j
 
         def relus(n):
             o, j = out_tile(n)
-            first, size = chunk_of[n]
-            k = n - first
-            for h in range(HB):
-                src = tp[first][:, k, DH * h : DH * (h + 1)]
-                c = HB * k + h
-                nc.scalar.activation(out=o[:, h, j, 0:DH], in_=src, func=ACT.Relu, scale=rc[first][:, c : c + 1])
-                nc.scalar.activation(
-                    out=o[:, h, j, DH : 2 * DH], in_=src, func=ACT.Relu, scale=rn[first][:, c : c + 1]
-                )
+            first = n - n % CHUNK
+            src = heads(tn[first][:, n - first, :])
+            nc.scalar.activation(out=o[:, :, j, 0:DH], in_=src, func=ACT.Relu)
+            nc.scalar.activation(out=o[:, :, j, DH : 2 * DH], in_=src, func=ACT.Relu, scale=-1.0)
 
         def v_final(n):
             o, j = out_tile(n)
-            first, size = chunk_of[n]
-            src = heads(tp[first][:, n - first, :])
-            r = rc[first][:, HB * (n - first) : HB * (n - first + 1)]
-            rneg = rn[first][:, HB * (n - first) : HB * (n - first + 1)]
-            nc.vector.scalar_tensor_tensor(
-                out=o[:, :, j, 0:DH], in0=src, scalar=0.0, in1=spread(r), op0=ALU.max, op1=ALU.mult
+            first = n - n % CHUNK
+            k = n - first
+            rneg = work.tile([P, HB], F32, name="rneg")
+            nc.vector.tensor_scalar(
+                out=rneg[:], in0=rc[first][:, HB * k : HB * (k + 1)], scalar1=-1.0, scalar2=None, op0=ALU.mult
             )
-            nc.vector.scalar_tensor_tensor(
-                out=o[:, :, j, DH : 2 * DH], in0=src, scalar=0.0, in1=spread(rneg), op0=ALU.min, op1=ALU.mult
-            )
+            half = HB // 2
+            for h0 in (0, half):
+                src = heads(tp[first][:, k, :])[:, h0 : h0 + half, :]
+                nc.vector.scalar_tensor_tensor(
+                    out=o[:, h0 : h0 + half, j, 0:DH],
+                    in0=src,
+                    scalar=0.0,
+                    in1=spread(rc[first][:, HB * k + h0 : HB * k + h0 + half], half),
+                    op0=ALU.max,
+                    op1=ALU.mult,
+                )
+                nc.vector.scalar_tensor_tensor(
+                    out=o[:, h0 : h0 + half, j, DH : 2 * DH],
+                    in0=src,
+                    scalar=0.0,
+                    in1=spread(rneg[:, h0 : h0 + half], half),
+                    op0=ALU.min,
+                    op1=ALU.mult,
+                )
 
-        def dest(grp):
-            b, cg = divmod(grp, NCG)
+        def store(b, cg, j0, nj):
             dst = out_0 if cg < NCG // 2 else out_1
             h0 = HB * (cg % (NCG // 2))
-            return dst, b, h0
-
-        def store(first, size, h_lo, h_n):
-            grp, j = divmod(first, J)
-            dst, b, h0 = dest(grp)
-            nc.sync.dma_start(
-                out=dst[b, h0 + h_lo : h0 + h_lo + h_n]
-                .rearrange("h (p j) f -> p h j f", j=J)[:, :, j : j + size, :]
-                .rearrange("p h j f -> p h (j f)"),
-                in_=o_sb[grp][:, h_lo : h_lo + h_n, j : j + size, :].rearrange("p h j f -> p h (j f)"),
-            )
+            nh = HB // STORE_SPLIT
+            for h in range(0, HB, nh):
+                nc.sync.dma_start(
+                    out=dst[b, h0 + h : h0 + h + nh]
+                    .rearrange("h (p j) f -> p h j f", j=J)[:, :, j0 : j0 + nj, :]
+                    .rearrange("p h j f -> p h (j f)"),
+                    in_=o_sb[(b, cg)][:, h : h + nh, j0 : j0 + nj, :].rearrange("p h j f -> p h (j f)"),
+                )
 
         def finish(n):
-            if n >= NU - V_FINAL:
+            if n >= nu - V_FINAL:
                 v_final(n)
             else:
                 relus(n)
-            if n in last_of:
-                first, size = last_of[n]
-                store(first, size, 0, HB // 2)
-                store(first, size, HB // 2, HB // 2)
+            b, cg, j = units[n]
+            nj = rows[(b, cg)]
+            if (j + 1) % nj == 0:
+                store(b, cg, j + 1 - nj, nj)
 
-        for t in range(LEAD_MM):
-            prep(t)
-            quant(t)
+        prep(0)
+        quant(0)
+        prep(1)
+        quant(1)
         for n in range(LEAD_MM):
             mm(n)
         for n in range(LEAD_SG):
             sign(n)
         pending = []
         served = 0
-        for n in range(NU + 2):
-            if n + LEAD_MM < B * J:
-                prep(n + LEAD_MM)
-                quant(n + LEAD_MM)
-            if n + LEAD_MM < NU:
+        for n in range(nu + 2):
+            if n + 2 < B * J:
+                prep(n + 2)
+                quant(n + 2)
+            if n + LEAD_MM < nu:
                 mm(n + LEAD_MM)
-            if n + LEAD_SG < NU:
+            if n + LEAD_SG < nu:
                 sign(n + LEAD_SG)
-            if n < NU:
+            if n < nu:
                 c_main(n)
-            ready = last_of.get(n - 2)
+            ready = n >= CHUNK + 1 and (n - 1) % CHUNK == 0
+            first = n - 1 - CHUNK
             if ready:
-                reduce(ready[0], ready[1])
-            if 1 <= n <= NU:
+                reduce(first)
+            if 1 <= n <= nu:
                 t_prime(n - 1)
-            if n < NU:
+            if n < nu:
                 c_wrap(n)
             for k in range(2 if len(pending) - served > J else 1):
                 if served < len(pending):
                     finish(pending[served])
                     served += 1
             if ready:
-                recip(ready[0], ready[1])
-                pending.extend(range(ready[0], ready[0] + ready[1]))
+                recip(first)
+                for m in range(first, first + CHUNK):
+                    if m < nu - V_FINAL:
+                        scale(m)
+                    pending.append(m)
         for n in pending[served:]:
             finish(n)

@@ -23,8 +23,9 @@ NG = D // 512
 HB = 8
 NCG = 2 * H // HB
 BANK = HB * DH
-CHUNK = 2
+CHUNKS = (2,) * 14 + (1, 1, 1, 1)
 V_FINAL = 1
+S_FINAL = 3
 LEAD_MM = 4
 LEAD_SG = 3
 N_WARM = 4
@@ -45,6 +46,14 @@ def tile_dpfpattention_pa_kernel(tc, x, w_qk_words, w_qk_scales, out_0, out_1):
     rows = {(b, cg): J for b in range(B) for cg in range(NCG)}
     rows[(1, 2)] = 2
     rows[(1, 3)] = 2
+    chunk_of = {}
+    last_of = {}
+    start = 0
+    for size in CHUNKS:
+        last_of[start + size - 1] = (start, size)
+        for n in range(start, start + size):
+            chunk_of[n] = (start, size)
+        start += size
     with ExitStack() as ctx:
         const = ctx.enter_context(tc.tile_pool(name="const", bufs=1))
         stage = ctx.enter_context(tc.tile_pool(name="stage", bufs=3))
@@ -54,7 +63,7 @@ def tile_dpfpattention_pa_kernel(tc, x, w_qk_words, w_qk_scales, out_0, out_1):
 
         x_sb, xq, xs, grouped = {}, {}, {}, {}
         ww, ws = {}, {}
-        u_ps, sg, cp, tp, tn, rc, sm, o_sb = {}, {}, {}, {}, {}, {}, {}, {}
+        u_ps, sg, cp, tp, tn, rc, rn, sm, o_sb = {}, {}, {}, {}, {}, {}, {}, {}, {}
 
         zero = const.tile([P, BANK], BF16, name="zero")
         nc.vector.memset(zero[:], 0.0)
@@ -165,9 +174,9 @@ def tile_dpfpattention_pa_kernel(tc, x, w_qk_words, w_qk_scales, out_0, out_1):
             )
 
         def t_prime(n):
-            first = n - n % CHUNK
+            first, size = chunk_of[n]
             if n == first:
-                tpt = work.tile([P, CHUNK, BANK], F32, name="tp")
+                tpt = work.tile([P, size, BANK], F32, name="tp")
                 tp[first] = tpt
             nc.vector.scalar_tensor_tensor(
                 out=tp[first][:, n - first, :],
@@ -178,8 +187,8 @@ def tile_dpfpattention_pa_kernel(tc, x, w_qk_words, w_qk_scales, out_0, out_1):
                 op1=ALU.mult,
             )
 
-        def reduce(first):
-            s = work.tile([P, CHUNK * HB], F32, name="sm")
+        def reduce(first, size):
+            s = work.tile([P, size * HB], F32, name="sm")
             nc.vector.tensor_reduce(
                 out=s[:],
                 in_=tp[first][:].rearrange("p k (h i) -> p (k h) i", i=DH),
@@ -189,19 +198,23 @@ def tile_dpfpattention_pa_kernel(tc, x, w_qk_words, w_qk_scales, out_0, out_1):
             )
             sm[first] = s
 
-        def recip(first):
-            r = work.tile([P, CHUNK * HB], F32, name="rc")
+        def recip(first, size):
+            r = work.tile([P, size * HB], F32, name="rc")
             nc.vector.reciprocal(out=r[:], in_=sm[first][:])
             rc[first] = r
+            if first >= nu - V_FINAL - S_FINAL:
+                rm = work.tile([P, size * HB], F32, name="rn")
+                nc.vector.tensor_scalar(out=rm[:], in0=r[:], scalar1=-1.0, scalar2=None, op0=ALU.mult)
+                rn[first] = rm
 
         def spread(r_ap, nh):
             return r_ap.unsqueeze(2).to_broadcast([P, nh, DH])
 
         def scale(n):
-            first = n - n % CHUNK
+            first, size = chunk_of[n]
             k = n - first
             if first not in tn:
-                t = work.tile([P, CHUNK, BANK], F32, name="tn")
+                t = work.tile([P, size, BANK], F32, name="tn")
                 tn[first] = t
             nc.gpsimd.tensor_tensor(
                 out=heads(tn[first][:, k, :]),
@@ -219,38 +232,37 @@ def tile_dpfpattention_pa_kernel(tc, x, w_qk_words, w_qk_scales, out_0, out_1):
 
         def relus(n):
             o, j = out_tile(n)
-            first = n - n % CHUNK
+            first, size = chunk_of[n]
             src = heads(tn[first][:, n - first, :])
             nc.scalar.activation(out=o[:, :, j, 0:DH], in_=src, func=ACT.Relu)
             nc.scalar.activation(out=o[:, :, j, DH : 2 * DH], in_=src, func=ACT.Relu, scale=-1.0)
 
-        def v_final(n):
+        def v_final(n, h0, nh):
             o, j = out_tile(n)
-            first = n - n % CHUNK
-            k = n - first
-            rneg = work.tile([P, HB], F32, name="rneg")
-            nc.vector.tensor_scalar(
-                out=rneg[:], in0=rc[first][:, HB * k : HB * (k + 1)], scalar1=-1.0, scalar2=None, op0=ALU.mult
+            src = heads(tp[n][:, 0, :])[:, h0 : h0 + nh, :]
+            nc.vector.scalar_tensor_tensor(
+                out=o[:, h0 : h0 + nh, j, 0:DH],
+                in0=src,
+                scalar=0.0,
+                in1=spread(rc[n][:, h0 : h0 + nh], nh),
+                op0=ALU.max,
+                op1=ALU.mult,
             )
-            half = HB // 2
-            for h0 in (0, half):
-                src = heads(tp[first][:, k, :])[:, h0 : h0 + half, :]
-                nc.vector.scalar_tensor_tensor(
-                    out=o[:, h0 : h0 + half, j, 0:DH],
-                    in0=src,
-                    scalar=0.0,
-                    in1=spread(rc[first][:, HB * k + h0 : HB * k + h0 + half], half),
-                    op0=ALU.max,
-                    op1=ALU.mult,
-                )
-                nc.vector.scalar_tensor_tensor(
-                    out=o[:, h0 : h0 + half, j, DH : 2 * DH],
-                    in0=src,
-                    scalar=0.0,
-                    in1=spread(rneg[:, h0 : h0 + half], half),
-                    op0=ALU.min,
-                    op1=ALU.mult,
-                )
+            nc.vector.scalar_tensor_tensor(
+                out=o[:, h0 : h0 + nh, j, DH : 2 * DH],
+                in0=src,
+                scalar=0.0,
+                in1=spread(rn[n][:, h0 : h0 + nh], nh),
+                op0=ALU.min,
+                op1=ALU.mult,
+            )
+
+        def s_final(n, h0, nh):
+            o, j = out_tile(n)
+            for h in range(h0, h0 + nh):
+                src = tp[n][:, 0, DH * h : DH * (h + 1)]
+                nc.scalar.activation(out=o[:, h, j, 0:DH], in_=src, func=ACT.Relu, scale=rc[n][:, h : h + 1])
+                nc.scalar.activation(out=o[:, h, j, DH : 2 * DH], in_=src, func=ACT.Relu, scale=rn[n][:, h : h + 1])
 
         def store(b, cg, j0, nj):
             dst = out_0 if cg < NCG // 2 else out_1
@@ -266,7 +278,10 @@ def tile_dpfpattention_pa_kernel(tc, x, w_qk_words, w_qk_scales, out_0, out_1):
 
         def finish(n):
             if n >= nu - V_FINAL:
-                v_final(n)
+                v_final(n, 0, HB // 2)
+                s_final(n, HB // 2, HB // 2)
+            elif n >= nu - V_FINAL - S_FINAL:
+                s_final(n, 0, HB)
             else:
                 relus(n)
             b, cg, j = units[n]
@@ -294,10 +309,9 @@ def tile_dpfpattention_pa_kernel(tc, x, w_qk_words, w_qk_scales, out_0, out_1):
                 sign(n + LEAD_SG)
             if n < nu:
                 c_main(n)
-            ready = n >= CHUNK + 1 and (n - 1) % CHUNK == 0
-            first = n - 1 - CHUNK
+            ready = last_of.get(n - 2)
             if ready:
-                reduce(first)
+                reduce(ready[0], ready[1])
             if 1 <= n <= nu:
                 t_prime(n - 1)
             if n < nu:
@@ -307,9 +321,9 @@ def tile_dpfpattention_pa_kernel(tc, x, w_qk_words, w_qk_scales, out_0, out_1):
                     finish(pending[served])
                     served += 1
             if ready:
-                recip(first)
-                for m in range(first, first + CHUNK):
-                    if m < nu - V_FINAL:
+                recip(ready[0], ready[1])
+                for m in range(ready[0], ready[0] + ready[1]):
+                    if m < nu - V_FINAL - S_FINAL:
                         scale(m)
                     pending.append(m)
         for n in pending[served:]:

@@ -65,15 +65,18 @@ def tile_dpfpattention_pa_kernel(tc, x, w_qk_words, w_qk_scales, out_0, out_1):
         ww, ws = {}, {}
         u_ps, sg, cp, tp, tn, rc, rn, sm, o_sb = {}, {}, {}, {}, {}, {}, {}, {}, {}
 
-        zero = const.tile([P, BANK], BF16, name="zero")
-        nc.vector.memset(zero[:], 0.0)
-        warm = const.tile([P, 1], F32, name="warm")
-        nc.scalar.activation(out=warm[:], in_=zero[:, 0:1], func=ACT.Sign)
-
-        for cg in range(NCG):
-            plane = const.tile([P, NG, BANK], U8, name="ws%d" % cg, align_bytes=64)
+        planes = []
+        for half in range(2):
+            plane = const.tile([P, NG, 2 * BANK], U8, name="ws%d" % half, align_bytes=64)
             nc.vector.memset(plane[:].bitcast(I32), 0)
-            ws[cg] = plane
+            planes.append(plane)
+            for c in range(2):
+                ws[2 * half + c] = plane[:, :, BANK * c : BANK * (c + 1)]
+            if half == 0:
+                zero = const.tile([P, BANK], BF16, name="zero")
+                nc.vector.memset(zero[:], 0.0)
+                warm = const.tile([P, 1], F32, name="warm")
+                nc.scalar.activation(out=warm[:], in_=zero[:, 0:1], func=ACT.Sign)
 
         ident = const.tile([P, P], F32, name="ident")
         make_identity(nc, ident[:])
@@ -84,14 +87,16 @@ def tile_dpfpattention_pa_kernel(tc, x, w_qk_words, w_qk_scales, out_0, out_1):
             nc.sync.dma_start(out=xt[:], in_=x[b].rearrange("(p j) k -> p j k", j=J)[:, j, :])
             x_sb[t] = xt
 
-        def load_w(cg):
+        def load_scales(half):
             for q in range(4):
                 nc.sync.dma_start(
-                    out=ws[cg][32 * q : 32 * q + 4, :, :].bitcast(I32),
-                    in_=w_qk_scales[:, 4 * q : 4 * q + 4, BANK * cg : BANK * (cg + 1)]
+                    out=planes[half][32 * q : 32 * q + 4, :, :].bitcast(I32),
+                    in_=w_qk_scales[:, 4 * q : 4 * q + 4, 2 * BANK * half : 2 * BANK * (half + 1)]
                     .rearrange("g r n -> r g n")
                     .bitcast(I32),
                 )
+
+        def load_w(cg):
             words = const.tile([P, NG, 2 * BANK], U8, name="ww%d" % cg, align_bytes=64)
             nc.sync.dma_start(
                 out=words[:].bitcast(I32),
@@ -100,13 +105,17 @@ def tile_dpfpattention_pa_kernel(tc, x, w_qk_words, w_qk_scales, out_0, out_1):
             ww[cg] = words
 
         load_x(0)
+        load_scales(0)
         load_w(0)
-        load_x(1)
         load_w(1)
-        for t in range(2, B * J):
-            load_x(t)
+        load_x(1)
+        load_x(2)
+        load_x(3)
+        load_scales(1)
         load_w(2)
         load_w(3)
+        for t in range(J, B * J):
+            load_x(t)
 
         dummy = psum.tile([P, BANK], F32, name="bank")
         for i in range(N_WARM):

@@ -309,9 +309,10 @@ def tile_dpfpattention_pa_kernel(tc, x, w_qk_words, w_qk_scales, out_0, out_1):
         pending = []
         served = 0
         for n in range(nu + 2):
-            if n + 2 < B * J:
-                prep(n + 2)
-                quant(n + 2)
+            t_next = n + 2 if n < 2 else n - 2
+            if n < 2 or J <= t_next < B * J:
+                prep(t_next)
+                quant(t_next)
             if n + LEAD_MM < nu:
                 mm(n + LEAD_MM)
             if n + LEAD_SG < nu:

@@ -105,10 +105,10 @@ def tile_dpfpattention_pa_kernel(tc, x, w_qk_words, w_qk_scales, out_0, out_1):
             ww[cg] = words
 
         load_x(0)
+        load_x(1)
         load_scales(0)
         load_w(0)
         load_w(1)
-        load_x(1)
         load_x(2)
         load_x(3)
         load_scales(1)

@@ -302,17 +302,19 @@ def tile_dpfpattention_pa_kernel(tc, x, w_qk_words, w_qk_scales, out_0, out_1):
         quant(0)
         prep(1)
         quant(1)
-        for n in range(LEAD_MM):
-            mm(n)
+        for t in range(2, J):
+            mm(2 * t - 4)
+            mm(2 * t - 3)
+            prep(t)
+            quant(t)
         for n in range(LEAD_SG):
             sign(n)
         pending = []
         served = 0
         for n in range(nu + 2):
-            t_next = n + 2 if n < 2 else n - 2
-            if n < 2 or J <= t_next < B * J:
-                prep(t_next)
-                quant(t_next)
+            if J <= n - 2 < B * J:
+                prep(n - 2)
+                quant(n - 2)
             if n + LEAD_MM < nu:
                 mm(n + LEAD_MM)
             if n + LEAD_SG < nu:

@@ -56,12 +56,12 @@ def tile_dpfpattention_pa_kernel(tc, x, w_qk_words, w_qk_scales, out_0, out_1):
         start += size
     with ExitStack() as ctx:
         const = ctx.enter_context(tc.tile_pool(name="const", bufs=1))
-        stage = ctx.enter_context(tc.tile_pool(name="stage", bufs=3))
+        stage = ctx.enter_context(tc.tile_pool(name="stage", bufs=4))
         work = ctx.enter_context(tc.tile_pool(name="work", bufs=4))
         outp = ctx.enter_context(tc.tile_pool(name="outp", bufs=4))
         psum = ctx.enter_context(tc.psum_pool(name="psum", bufs=8))
 
-        x_sb, xq, xs, grouped = {}, {}, {}, {}
+        x_sb, xq, xs, grouped, turned = {}, {}, {}, {}, {}
         ww, ws = {}, {}
         u_ps, sg, cp, tp, tn, rc, rn, sm, o_sb = {}, {}, {}, {}, {}, {}, {}, {}, {}
 
@@ -121,18 +121,25 @@ def tile_dpfpattention_pa_kernel(tc, x, w_qk_words, w_qk_scales, out_0, out_1):
         for i in range(N_WARM):
             nc.tensor.matmul(out=dummy[:], lhsT=zero[:, 0:P], rhs=zero[:], start=True, stop=True)
 
-        def prep(t):
+        def turn(t):
             words = x_sb[t][:].bitcast(F32)
             xT = psum.tile([P, 2 * NG, P], F32, name="bank")
             for g in range(NG):
                 for u in range(2):
                     nc.tensor.transpose(xT[:, 2 * g + u, :], words[:, 256 * g + u : 256 * (g + 1) : 2], ident[:])
+            turned[t] = xT
+
+        def group(t):
             gr = stage.tile([P, NG * 512], BF16, name="gr", align_bytes=64)
             nc.scalar.copy(
                 out=gr[:].bitcast(F32).rearrange("p (g r u) -> p g r u", g=NG, u=2),
-                in_=xT[:].rearrange("p (g u) r -> p g r u", u=2),
+                in_=turned[t][:].rearrange("p (g u) r -> p g r u", u=2),
             )
             grouped[t] = gr
+
+        def prep(t):
+            turn(t)
+            group(t)
 
         def quant(t):
             codes = const.tile([P, NG * P], U32, name="xq%d" % t, align_bytes=64)
@@ -312,9 +319,12 @@ def tile_dpfpattention_pa_kernel(tc, x, w_qk_words, w_qk_scales, out_0, out_1):
         pending = []
         served = 0
         for n in range(nu + 2):
+            if J <= n - 1 < B * J:
+                turn(n - 1)
             if J <= n - 2 < B * J:
-                prep(n - 2)
-                quant(n - 2)
+                group(n - 2)
+            if J <= n - 4 < B * J:
+                quant(n - 4)
             if n + LEAD_MM < nu:
                 mm(n + LEAD_MM)
             if n + LEAD_SG < nu:

@@ -313,9 +313,15 @@ def tile_dpfpattention_pa_kernel(tc, x, w_qk_words, w_qk_scales, out_0, out_1):
             mm(2 * t - 4)
             mm(2 * t - 3)
             prep(t)
-            quant(t)
         for n in range(LEAD_SG):
             sign(n)
+        mm_in_step = {}
+        sign_in_step = {}
+        for k in range(LEAD_MM, nu):
+            step = max(k - LEAD_MM, k // 2 if k < 2 * J else 0)
+            mm_in_step.setdefault(step, []).append(k)
+            sign_in_step.setdefault(max(k - LEAD_SG, step), []).append(k)
+        sign_in_step.setdefault(0, []).append(LEAD_SG)
         pending = []
         served = 0
         for n in range(nu + 2):
@@ -325,10 +331,12 @@ def tile_dpfpattention_pa_kernel(tc, x, w_qk_words, w_qk_scales, out_0, out_1):
                 group(n - 2)
             if J <= n - 4 < B * J:
                 quant(n - 4)
-            if n + LEAD_MM < nu:
-                mm(n + LEAD_MM)
-            if n + LEAD_SG < nu:
-                sign(n + LEAD_SG)
+            if 2 <= n < J:
+                quant(n)
+            for k in mm_in_step.get(n, []):
+                mm(k)
+            for k in sign_in_step.get(n, []):
+                sign(k)
             if n < nu:
                 c_main(n)
             ready = last_of.get(n - 2)

@@ -45,7 +45,7 @@ def tile_dpfpattention_pa_kernel(tc, x, w_qk_words, w_qk_scales, out_0, out_1):
     nu = len(units)
     rows = {(b, cg): J for b in range(B) for cg in range(NCG)}
     rows[(1, 2)] = 2
-    rows[(1, 3)] = 2
+    rows[(1, 3)] = 1
     chunk_of = {}
     last_of = {}
     start = 0
@@ -283,7 +283,7 @@ def tile_dpfpattention_pa_kernel(tc, x, w_qk_words, w_qk_scales, out_0, out_1):
         def store(b, cg, j0, nj):
             dst = out_0 if cg < NCG // 2 else out_1
             h0 = HB * (cg % (NCG // 2))
-            nh = HB // STORE_SPLIT
+            nh = {J: HB // STORE_SPLIT, 2: HB // 2, 1: HB if j0 < 2 else HB // 2}[nj]
             for h in range(0, HB, nh):
                 nc.sync.dma_start(
                     out=dst[b, h0 + h : h0 + h + nh]
@@ -295,7 +295,10 @@ def tile_dpfpattention_pa_kernel(tc, x, w_qk_words, w_qk_scales, out_0, out_1):
         def finish(n):
             if n >= nu - V_FINAL:
                 v_final(n, 0, HB // 2)
-                s_final(n, HB // 2, HB // 2)
+                v_final(n, HB // 2, HB // 2)
+            elif n == nu - V_FINAL - 1:
+                s_final(n, 0, HB // 2)
+                v_final(n, HB // 2, HB // 2)
             elif n >= nu - V_FINAL - S_FINAL:
                 s_final(n, 0, HB)
             else:

@@ -23,7 +23,7 @@ NG = D // 512
 HB = 8
 NCG = 2 * H // HB
 BANK = HB * DH
-CHUNKS = (2,) * 14 + (1, 1, 1, 1)
+CHUNKS = (2,) * 8 + (1,) * 16
 V_FINAL = 1
 S_FINAL = 3
 LEAD_MM = 4

@@ -148,6 +148,31 @@ def tile_dpfpattention_pa_kernel(tc, x, w_qk_words, w_qk_scales, out_0, out_1):
             xq[t] = codes
             xs[t] = scales
 
+        def first_tile():
+            words = x_sb[0][:].bitcast(F32)
+            gr = stage.tile([P, NG * 512], BF16, name="gr", align_bytes=64)
+            codes = const.tile([P, NG * P], U32, name="xq0", align_bytes=64)
+            scales = const.tile([P, NG * P], U8, name="xs0", align_bytes=64)
+            halves = []
+            for g in range(NG):
+                xT = psum.tile([P, 2, P], F32, name="bank")
+                for u in range(2):
+                    nc.tensor.transpose(xT[:, u, :], words[:, 256 * g + u : 256 * (g + 1) : 2], ident[:])
+                halves.append(xT)
+            for g in range(NG):
+                nc.scalar.copy(
+                    out=gr[:, 512 * g : 512 * (g + 1)].bitcast(F32).rearrange("p (r u) -> p r u", u=2),
+                    in_=halves[g][:].rearrange("p u r -> p r u"),
+                )
+            for g in range(NG):
+                nc.vector.quantize_mx(
+                    out=codes[:, P * g : P * (g + 1)].bitcast(E5M2X4),
+                    scales=scales[:, P * g : P * (g + 1)],
+                    in_=gr[:, 512 * g : 512 * (g + 1)],
+                )
+            xq[0] = codes
+            xs[0] = scales
+
         def mm(n):
             b, cg, j = units[n]
             t = J * b + j
@@ -308,8 +333,7 @@ def tile_dpfpattention_pa_kernel(tc, x, w_qk_words, w_qk_scales, out_0, out_1):
             if (j + 1) % nj == 0:
                 store(b, cg, j + 1 - nj, nj)
 
-        prep(0)
-        quant(0)
+        first_tile()
         prep(1)
         quant(1)
         for t in range(2, J):

from contextlib import ExitStack

import concourse.mybir as mybir
from concourse.masks import make_identity

B, N, D, H, DH = 2, 512, 1024, 16, 64
FLOPS = 2 * B * N * D * 2 * H * DH

F32 = mybir.dt.float32
BF16 = mybir.dt.bfloat16
U32 = mybir.dt.uint32
U8 = mybir.dt.uint8
I32 = mybir.dt.int32
E5M2X4 = mybir.dt.float8_e5m2_x4
E2M1X4 = mybir.dt.float4_e2m1fn_x4
ACT = mybir.ActivationFunctionType
ALU = mybir.AluOpType
AX = mybir.AxisListType

P = 128
J = 4
NG = D // 512
HB = 8
NCG = 2 * H // HB
BANK = HB * DH
CHUNKS = (2,) * 8 + (1,) * 16
V_FINAL = 1
S_FINAL = 3
LEAD_MM = 4
LEAD_SG = 3
N_WARM = 4
STORE_SPLIT = 4


def unit_order():
    units = [(0, cg, j) for j in range(J) for cg in (0, 1)]
    units += [(0, cg, j) for cg in (2, 3) for j in range(J)]
    units += [(1, cg, j) for cg in range(NCG) for j in range(J)]
    return units


def tile_dpfpattention_pa_kernel(tc, x, w_qk_words, w_qk_scales, out_0, out_1):
    nc = tc.nc
    units = unit_order()
    nu = len(units)
    rows = {(b, cg): J for b in range(B) for cg in range(NCG)}
    rows[(1, 2)] = 2
    rows[(1, 3)] = 1
    chunk_of = {}
    last_of = {}
    start = 0
    for size in CHUNKS:
        last_of[start + size - 1] = (start, size)
        for n in range(start, start + size):
            chunk_of[n] = (start, size)
        start += size
    with ExitStack() as ctx:
        const = ctx.enter_context(tc.tile_pool(name="const", bufs=1))
        stage = ctx.enter_context(tc.tile_pool(name="stage", bufs=4))
        work = ctx.enter_context(tc.tile_pool(name="work", bufs=4))
        outp = ctx.enter_context(tc.tile_pool(name="outp", bufs=4))
        psum = ctx.enter_context(tc.psum_pool(name="psum", bufs=8))

        x_sb, xq, xs, grouped, turned = {}, {}, {}, {}, {}
        ww, ws = {}, {}
        u_ps, sg, cp, tp, tn, rc, rn, sm, o_sb = {}, {}, {}, {}, {}, {}, {}, {}, {}

        planes = []
        for half in range(2):
            plane = const.tile([P, NG, 2 * BANK], U8, name="ws%d" % half, align_bytes=64)
            nc.vector.memset(plane[:].bitcast(I32), 0)
            planes.append(plane)
            for c in range(2):
                ws[2 * half + c] = plane[:, :, BANK * c : BANK * (c + 1)]
            if half == 0:
                zero = const.tile([P, BANK], BF16, name="zero")
                nc.vector.memset(zero[:], 0.0)
                warm = const.tile([P, 1], F32, name="warm")
                nc.scalar.activation(out=warm[:], in_=zero[:, 0:1], func=ACT.Sign)

        ident = const.tile([P, P], F32, name="ident")
        make_identity(nc, ident[:])

        def load_x(t):
            b, j = divmod(t, J)
            xt = const.tile([P, D], BF16, name="x%d" % t)
            nc.sync.dma_start(out=xt[:], in_=x[b].rearrange("(p j) k -> p j k", j=J)[:, j, :])
            x_sb[t] = xt

        def load_scales(half):
            for q in range(4):
                nc.sync.dma_start(
                    out=planes[half][32 * q : 32 * q + 4, :, :].bitcast(I32),
                    in_=w_qk_scales[:, 4 * q : 4 * q + 4, 2 * BANK * half : 2 * BANK * (half + 1)]
                    .rearrange("g r n -> r g n")
                    .bitcast(I32),
                )

        def load_w(cg):
            words = const.tile([P, NG, 2 * BANK], U8, name="ww%d" % cg, align_bytes=64)
            nc.sync.dma_start(
                out=words[:].bitcast(I32),
                in_=w_qk_words[:, :, 2 * BANK * cg : 2 * BANK * (cg + 1)].rearrange("g p n -> p g n").bitcast(I32),
            )
            ww[cg] = words

        load_x(0)
        load_x(1)
        load_scales(0)
        load_w(0)
        load_w(1)
        load_x(2)
        load_x(3)
        load_scales(1)
        load_w(2)
        load_w(3)
        for t in range(J, B * J):
            load_x(t)

        dummy = psum.tile([P, BANK], F32, name="bank")
        for i in range(N_WARM):
            nc.tensor.matmul(out=dummy[:], lhsT=zero[:, 0:P], rhs=zero[:], start=True, stop=True)

        def turn(t):
            words = x_sb[t][:].bitcast(F32)
            xT = psum.tile([P, 2 * NG, P], F32, name="bank")
            for g in range(NG):
                for u in range(2):
                    nc.tensor.transpose(xT[:, 2 * g + u, :], words[:, 256 * g + u : 256 * (g + 1) : 2], ident[:])
            turned[t] = xT

        def group(t):
            gr = stage.tile([P, NG * 512], BF16, name="gr", align_bytes=64)
            nc.scalar.copy(
                out=gr[:].bitcast(F32).rearrange("p (g r u) -> p g r u", g=NG, u=2),
                in_=turned[t][:].rearrange("p (g u) r -> p g r u", u=2),
            )
            grouped[t] = gr

        def prep(t):
            turn(t)
            group(t)

        def quant(t):
            codes = const.tile([P, NG * P], U32, name="xq%d" % t, align_bytes=64)
            scales = const.tile([P, NG * P], U8, name="xs%d" % t, align_bytes=64)
            nc.vector.quantize_mx(out=codes[:].bitcast(E5M2X4), scales=scales[:], in_=grouped[t][:])
            xq[t] = codes
            xs[t] = scales

        def first_tile():
            words = x_sb[0][:].bitcast(F32)
            gr = stage.tile([P, NG * 512], BF16, name="gr", align_bytes=64)
            codes = const.tile([P, NG * P], U32, name="xq0", align_bytes=64)
            scales = const.tile([P, NG * P], U8, name="xs0", align_bytes=64)
            halves = []
            for g in range(NG):
                xT = psum.tile([P, 2, P], F32, name="bank")
                for u in range(2):
                    nc.tensor.transpose(xT[:, u, :], words[:, 256 * g + u : 256 * (g + 1) : 2], ident[:])
                halves.append(xT)
            for g in range(NG):
                nc.scalar.copy(
                    out=gr[:, 512 * g : 512 * (g + 1)].bitcast(F32).rearrange("p (r u) -> p r u", u=2),
                    in_=halves[g][:].rearrange("p u r -> p r u"),
                )
            for g in range(NG):
                nc.vector.quantize_mx(
                    out=codes[:, P * g : P * (g + 1)].bitcast(E5M2X4),
                    scales=scales[:, P * g : P * (g + 1)],
                    in_=gr[:, 512 * g : 512 * (g + 1)],
                )
            xq[0] = codes
            xs[0] = scales

        def mm(n):
            b, cg, j = units[n]
            t = J * b + j
            acc = psum.tile([P, BANK], F32, name="bank")
            for g in range(NG):
                nc.tensor.matmul_mx(
                    out=acc[:],
                    lhsT=xq[t][:, P * g : P * (g + 1)].bitcast(E5M2X4),
                    lhsT_scale=xs[t][:, P * g : P * (g + 1)],
                    rhs=ww[cg][:, g, :].bitcast(E2M1X4),
                    rhs_scale=ws[cg][:, g, :],
                    start=(g == 0),
                    stop=(g == NG - 1),
                )
            u_ps[n] = acc

        def sign(n):
            s = work.tile([P, BANK], F32, name="sg", bufs=LEAD_SG + 3)
            nc.scalar.activation(out=s[:], in_=u_ps[n][:], func=ACT.Sign)
            sg[n] = s

        def heads(ap):
            return ap.rearrange("p (h i) -> p h i", i=DH)

        def c_main(n):
            c = work.tile([P, BANK], F32, name="cp")
            cp[n] = c
            nc.vector.tensor_tensor(
                out=c[:, 1:BANK], in0=u_ps[n][:, 0 : BANK - 1], in1=sg[n][:, 1:BANK], op=ALU.mult
            )

        def c_wrap(n):
            nc.vector.scalar_tensor_tensor(
                out=heads(cp[n][:])[:, :, 0:1],
                in0=heads(u_ps[n][:])[:, :, DH - 1 : DH],
                scalar=-1.0,
                in1=heads(sg[n][:])[:, :, 0:1],
                op0=ALU.mult,
                op1=ALU.mult,
            )

        def t_prime(n):
            first, size = chunk_of[n]
            if n == first:
                tpt = work.tile([P, size, BANK], F32, name="tp")
                tp[first] = tpt
            nc.vector.scalar_tensor_tensor(
                out=tp[first][:, n - first, :],
                in0=cp[n][:],
                scalar=0.0,
                in1=u_ps[n][:],
                op0=ALU.max,
                op1=ALU.mult,
            )

        def reduce(first, size):
            s = work.tile([P, size * HB], F32, name="sm")
            nc.vector.tensor_reduce(
                out=s[:],
                in_=tp[first][:].rearrange("p k (h i) -> p (k h) i", i=DH),
                axis=AX.X,
                op=ALU.add,
                apply_absolute_value=True,
            )
            sm[first] = s

        def recip(first, size):
            r = work.tile([P, size * HB], F32, name="rc")
            nc.vector.reciprocal(out=r[:], in_=sm[first][:])
            rc[first] = r
            if first >= nu - V_FINAL - S_FINAL:
                rm = work.tile([P, size * HB], F32, name="rn")
                nc.vector.tensor_scalar(out=rm[:], in0=r[:], scalar1=-1.0, scalar2=None, op0=ALU.mult)
                rn[first] = rm

        def spread(r_ap, nh):
            return r_ap.unsqueeze(2).to_broadcast([P, nh, DH])

        def scale(n):
            first, size = chunk_of[n]
            k = n - first
            if first not in tn:
                t = work.tile([P, size, BANK], F32, name="tn")
                tn[first] = t
            nc.gpsimd.tensor_tensor(
                out=heads(tn[first][:, k, :]),
                in0=heads(tp[first][:, k, :]),
                in1=spread(rc[first][:, HB * k : HB * (k + 1)], HB),
                op=ALU.mult,
            )

        def out_tile(n):
            b, cg, j = units[n]
            if j == 0:
                o = outp.tile([P, HB, J, 2 * DH], F32, name="o")
                o_sb[(b, cg)] = o
            return o_sb[(b, cg)], j

        def relus(n):
            o, j = out_tile(n)
            first, size = chunk_of[n]
            src = heads(tn[first][:, n - first, :])
            nc.scalar.activation(out=o[:, :, j, 0:DH], in_=src, func=ACT.Relu)
            nc.scalar.activation(out=o[:, :, j, DH : 2 * DH], in_=src, func=ACT.Relu, scale=-1.0)

        def v_final(n, h0, nh):
            o, j = out_tile(n)
            src = heads(tp[n][:, 0, :])[:, h0 : h0 + nh, :]
            nc.vector.scalar_tensor_tensor(
                out=o[:, h0 : h0 + nh, j, 0:DH],
                in0=src,
                scalar=0.0,
                in1=spread(rc[n][:, h0 : h0 + nh], nh),
                op0=ALU.max,
                op1=ALU.mult,
            )
            nc.vector.scalar_tensor_tensor(
                out=o[:, h0 : h0 + nh, j, DH : 2 * DH],
                in0=src,
                scalar=0.0,
                in1=spread(rn[n][:, h0 : h0 + nh], nh),
                op0=ALU.min,
                op1=ALU.mult,
            )

        def s_final(n, h0, nh):
            o, j = out_tile(n)
            for h in range(h0, h0 + nh):
                src = tp[n][:, 0, DH * h : DH * (h + 1)]
                nc.scalar.activation(out=o[:, h, j, 0:DH], in_=src, func=ACT.Relu, scale=rc[n][:, h : h + 1])
                nc.scalar.activation(out=o[:, h, j, DH : 2 * DH], in_=src, func=ACT.Relu, scale=rn[n][:, h : h + 1])

        def store(b, cg, j0, nj):
            dst = out_0 if cg < NCG // 2 else out_1
            h0 = HB * (cg % (NCG // 2))
            nh = {J: HB // STORE_SPLIT, 2: HB // 2, 1: HB if j0 < 2 else HB // 2}[nj]
            for h in range(0, HB, nh):
                nc.sync.dma_start(
                    out=dst[b, h0 + h : h0 + h + nh]
                    .rearrange("h (p j) f -> p h j f", j=J)[:, :, j0 : j0 + nj, :]
                    .rearrange("p h j f -> p h (j f)"),
                    in_=o_sb[(b, cg)][:, h : h + nh, j0 : j0 + nj, :].rearrange("p h j f -> p h (j f)"),
                )

        def finish(n):
            if n >= nu - V_FINAL:
                v_final(n, 0, HB // 2)
                v_final(n, HB // 2, HB // 2)
            elif n == nu - V_FINAL - 1:
                s_final(n, 0, HB // 2)
                v_final(n, HB // 2, HB // 2)
            elif n >= nu - V_FINAL - S_FINAL:
                s_final(n, 0, HB)
            else:
                relus(n)
            b, cg, j = units[n]
            nj = rows[(b, cg)]
            if (j + 1) % nj == 0:
                store(b, cg, j + 1 - nj, nj)

        first_tile()
        prep(1)
        quant(1)
        for t in range(2, J):
            mm(2 * t - 4)
            mm(2 * t - 3)
            prep(t)
        for n in range(LEAD_SG):
            sign(n)
        mm_in_step = {}
        sign_in_step = {}
        for k in range(LEAD_MM, nu):
            step = max(k - LEAD_MM, k // 2 if k < 2 * J else 0)
            mm_in_step.setdefault(step, []).append(k)
            sign_in_step.setdefault(max(k - LEAD_SG, step), []).append(k)
        sign_in_step.setdefault(0, []).append(LEAD_SG)
        pending = []
        served = 0
        for n in range(nu + 2):
            if J <= n - 1 < B * J:
                turn(n - 1)
            if J <= n - 2 < B * J:
                group(n - 2)
            if J <= n - 4 < B * J:
                quant(n - 4)
            if 2 <= n < J:
                quant(n)
            for k in mm_in_step.get(n, []):
                mm(k)
            for k in sign_in_step.get(n, []):
                sign(k)
            if n < nu:
                c_main(n)
            ready = last_of.get(n - 2)
            if ready:
                reduce(ready[0], ready[1])
            if 1 <= n <= nu:
                t_prime(n - 1)
            if n < nu:
                c_wrap(n)
            for k in range(2 if len(pending) - served > J else 1):
                if served < len(pending):
                    finish(pending[served])
                    served += 1
            if ready:
                recip(ready[0], ready[1])
                for m in range(ready[0], ready[0] + ready[1]):
                    if m < nu - V_FINAL - S_FINAL:
                        scale(m)
                    pending.append(m)
        for n in pending[served:]:
            finish(n)
